import numpy as np
import ml_dtypes


def mxq(x, axis, fmt="e4m3"):
    dtype, down = {"e4m3": (ml_dtypes.float8_e4m3fn, 7), "e5m2": (ml_dtypes.float8_e5m2, 14)}[fmt]
    v = np.moveaxis(np.asarray(x, np.float32).astype(ml_dtypes.bfloat16).astype(np.float64), axis, -1)
    blocks = v.reshape(v.shape[:-1] + (-1, 32))
    amax = np.abs(blocks).max(-1, keepdims=True)
    byte = np.maximum(np.where(amax > 0, np.frexp(amax)[1] - 1 + 127, 0) - down, 1)
    scale = np.exp2(byte - 127.0)
    codes = (blocks / scale).astype(np.float32).astype(dtype).astype(np.float64)
    return np.moveaxis((codes * scale).reshape(v.shape), -1, axis)


WIDE = False


def mx_kscale(k):
    if not WIDE:
        return np.ones(k)
    levels = np.array([10, -10, 5, -5, 0])
    a = np.random.permutation(np.resize(levels, k // 512 * 4)).reshape(k // 512, 4)
    idx = np.arange(k)
    return np.exp2(a[idx // 512, idx % 128 // 32])


BF16 = ml_dtypes.bfloat16


def bf(x):
    return np.asarray(x, np.float32).astype(BF16)


def f64(x):
    return np.asarray(x).astype(np.float64)


B, L, E, H, HD, F, G = 4, 128, 1024, 8, 128, 2048, 2048


def sigmoid(v):
    return 1.0 / (1.0 + np.exp(-v))


def setup_inputs():
    s, t = mx_kscale(E), mx_kscale(F)
    return {"h_ffn": bf(np.random.standard_normal((B, L, E)) * s),
            "w1": bf(np.random.standard_normal((E, F)) / np.sqrt(E) / s[:, None] * t),
            "b1": bf(0.2 * np.random.standard_normal(F) * t),
            "wg": bf(np.random.standard_normal((F, G)) / np.sqrt(F) / t[:, None]),
            "bg": bf(0.2 * np.random.standard_normal(G)),
            "wl": bf(np.random.standard_normal((F, G)) / np.sqrt(F) / t[:, None]),
            "bl": bf(0.2 * np.random.standard_normal(G)),
            "beta": bf(1.5 + 0.1 * np.random.standard_normal(1))}


def reference(h_ffn, w1, b1, wg, bg, wl, bl, beta):
    u = (mxq(f64(h_ffn), 2, "e4m3") @ mxq(f64(w1), 0, "e4m3")) + f64(b1)
    uq = mxq(u, 2, "e4m3")
    gate = (uq @ mxq(f64(wg), 0, "e4m3")) + f64(bg)
    lin = (uq @ mxq(f64(wl), 0, "e4m3")) + f64(bl)
    return gate * sigmoid(f64(beta) * gate) * lin

@@ -1,0 +1,307 @@
+from contextlib import ExitStack
+
+import concourse.mybir as mybir
+from concourse.masks import make_identity
+
+BF16 = mybir.dt.bfloat16
+F32 = mybir.dt.float32
+U32 = mybir.dt.uint32
+U8 = mybir.dt.uint8
+FP8X4 = mybir.dt.float8_e4m3fn_x4
+ACT = mybir.ActivationFunctionType
+ALU = mybir.AluOpType
+
+P = 128
+PACK = 4
+K_PASS = P * PACK
+
+BATCH = 4
+TOKENS = BATCH * P
+E = 1024
+F = 2048
+G = 2048
+E_PASSES = E // K_PASS
+F_PASSES = F // K_PASS
+
+QUANT = 4096
+WORDS = QUANT // PACK
+STRIPS_PER_LOAD = 4
+RAW = STRIPS_PER_LOAD * QUANT
+RAW_BUFS = 3
+BANKS = 8
+STORE = 512
+TILES_PER_STRIP = WORDS // F_PASSES // P
+
+QUANTISE_LAG = 1
+MULTIPLY_LAG = 2
+FINISH_LAG = 3
+TURN_LAG = 4
+
+FLOPS = 2 * TOKENS * E * F + 2 * 2 * TOKENS * F * G
+
+
+def tile_llamaselfattentionblock_pb_kernel(tc, h_ffn, w1, b1, wg, bg, wl, bl, beta, out):
+    nc = tc.nc
+    with ExitStack() as ctx:
+        const = ctx.enter_context(tc.tile_pool(name="const", bufs=1))
+        raw_pool = ctx.enter_context(tc.tile_pool(name="raw", bufs=RAW_BUFS))
+        grouped_pool = ctx.enter_context(tc.tile_pool(name="grouped", bufs=3))
+        strip_pool = ctx.enter_context(tc.tile_pool(name="strip", bufs=4))
+        u_pool = ctx.enter_context(tc.tile_pool(name="u", bufs=2))
+        swish_pool = ctx.enter_context(tc.tile_pool(name="swish", bufs=10))
+        work = ctx.enter_context(tc.tile_pool(name="work", bufs=4))
+        out_pool = ctx.enter_context(tc.tile_pool(name="out", bufs=2))
+        psum = ctx.enter_context(tc.psum_pool(name="psum", bufs=BANKS))
+        ctx.enter_context(tc.manual_schedule())
+        loads = [("u", w1, 0)]
+        for half in range(2):
+            loads.append(("gate", wg, half))
+            loads.append(("lin", wl, half))
+        n_strips = len(loads) * STRIPS_PER_LOAD
+
+        def kind(i):
+            return loads[i // STRIPS_PER_LOAD][0] if 0 <= i < n_strips else "none"
+
+        raw_of = {}
+        grouped_of = {}
+        words_of = {}
+        scales_of = {}
+        acc_of = {}
+        sig_of = {}
+        swish_of = {}
+        prod_of = {}
+        turned_of = {}
+        out_of = {}
+
+        def load(s):
+            w, half = loads[s][1], loads[s][2]
+            rows = w.shape[0] // P
+            width = RAW // rows
+            raw = raw_pool.tile([P, rows, width], BF16, tag="raw")
+            cuts = max(1, STRIPS_PER_LOAD >> s)
+            piece = width // cuts
+            for cut in range(cuts):
+                first = half * width + cut * piece
+                nc.sync.dma_start(
+                    out=raw[:, :, cut * piece : (cut + 1) * piece],
+                    in_=w[:, first : first + piece].rearrange("(r p) n -> p r n", p=P),
+                )
+            raw_of[s] = raw
+
+        def regroup(i):
+            s, q = divmod(i, STRIPS_PER_LOAD)
+            raw = raw_of[s]
+            passes = raw.shape[1] // PACK
+            n = WORDS // passes
+            vector_passes = 0 if kind(i - FINISH_LAG) == "u" else passes // 2
+            grouped = grouped_pool.tile([P, passes, n, PACK], BF16, align_bytes=64, tag="grouped")
+            for g in range(passes):
+                copy = nc.vector.tensor_copy if g < vector_passes else nc.scalar.copy
+                copy(
+                    out=grouped[:, g, :, :].rearrange("p (c i) t -> p c t i", i=4),
+                    in_=raw[:, g * PACK : (g + 1) * PACK, q * n : (q + 1) * n].rearrange("p t (c i) -> p c t i", i=4),
+                )
+            grouped_of[i] = grouped
+            if q == STRIPS_PER_LOAD - 1 and s + RAW_BUFS < len(loads):
+                load(s + RAW_BUFS)
+
+        def quantise(i):
+            grouped = grouped_of[i]
+            passes, n = grouped.shape[1], grouped.shape[2]
+            words = strip_pool.tile([P, passes, n], U32, align_bytes=64, tag="words")
+            scales = strip_pool.tile([P, passes, n], U8, align_bytes=64, tag="scales")
+            nc.vector.quantize_mx(
+                out=words[:].rearrange("p g n -> p (g n)").bitcast(FP8X4),
+                scales=scales[:].rearrange("p g n -> p (g n)"),
+                in_=grouped[:].rearrange("p g n t -> p (g n t)"),
+            )
+            words_of[i] = words
+            scales_of[i] = scales
+
+        def column_tile(i, j):
+            s, q = divmod(i, STRIPS_PER_LOAD)
+            return (loads[s][2] * STRIPS_PER_LOAD + q) * TILES_PER_STRIP + j
+
+        def multiply(i):
+            words, scales = words_of[i], scales_of[i]
+            banks = []
+            if kind(i) == "u":
+                for b in range(BATCH):
+                    tokens = slice(b * P, (b + 1) * P)
+                    u_acc = psum.tile([P, PACK, P], F32, tag="bank")
+                    for t in range(PACK):
+                        features = slice(t * P, (t + 1) * P)
+                        for c in range(E_PASSES):
+                            nc.tensor.matmul_mx(
+                                out=u_acc[:, t, :],
+                                lhsT=words[:, c, features].bitcast(FP8X4),
+                                lhsT_scale=scales[:, c, features],
+                                rhs=h_words[:, c, tokens].bitcast(FP8X4),
+                                rhs_scale=h_scales[:, c, tokens],
+                                start=(c == 0),
+                                stop=(c == E_PASSES - 1),
+                            )
+                    banks.append(u_acc)
+            else:
+                for j in range(TILES_PER_STRIP):
+                    cols = slice(j * P, (j + 1) * P)
+                    acc = psum.tile([P, TOKENS], F32, tag="bank")
+                    for g in range(F_PASSES):
+                        nc.tensor.matmul_mx(
+                            out=acc[:],
+                            lhsT=words[:, g, cols].bitcast(FP8X4),
+                            lhsT_scale=scales[:, g, cols],
+                            rhs=u_words[:, g, :].bitcast(FP8X4),
+                            rhs_scale=u_scales[:, g, :],
+                            start=(g == 0),
+                            stop=(g == F_PASSES - 1),
+                        )
+                    banks.append(acc)
+            acc_of[i] = banks
+
+        def sigmoid(i):
+            sigs = []
+            for j in range(TILES_PER_STRIP):
+                m = column_tile(i, j)
+                sig = work.tile([P, TOKENS], F32, tag="sig")
+                nc.scalar.activation(
+                    out=sig[:],
+                    in_=acc_of[i][j][:],
+                    func=ACT.Sigmoid,
+                    bias=beta_bg_cols[:, m : m + 1],
+                    scale=beta_col[:, 0:1],
+                )
+                sigs.append(sig)
+            sig_of[i] = sigs
+
+        def finish(i):
+            if kind(i) == "u":
+                u_grouped = u_pool.tile([P, TOKENS, PACK], BF16, align_bytes=64)
+                for b in range(BATCH):
+                    nc.vector.tensor_tensor(
+                        out=u_grouped[:, b * P : (b + 1) * P, :],
+                        in0=acc_of[i][b][:].rearrange("p t r -> p r t"),
+                        in1=b1_cols[:, i * PACK : (i + 1) * PACK].unsqueeze(1).to_broadcast([P, P, PACK]),
+                        op=ALU.add,
+                    )
+                nc.vector.quantize_mx(
+                    out=u_words[:, i, :].bitcast(FP8X4),
+                    scales=u_scales[:, i, :],
+                    in_=u_grouped[:].rearrange("p r t -> p (r t)"),
+                )
+            elif kind(i) == "gate":
+                swishes = []
+                for j in range(TILES_PER_STRIP):
+                    m = column_tile(i, j)
+                    swish = swish_pool.tile([P, TOKENS], F32)
+                    nc.vector.scalar_tensor_tensor(
+                        out=swish[:], in0=acc_of[i][j][:], scalar=bg_cols[:, m : m + 1], in1=sig_of[i][j][:],
+                        op0=ALU.add, op1=ALU.mult,
+                    )
+                    swishes.append(swish)
+                swish_of[i] = swishes
+            else:
+                prods = []
+                for j in range(TILES_PER_STRIP):
+                    m = column_tile(i, j)
+                    prod = work.tile([P, TOKENS], F32, tag="prod")
+                    nc.vector.scalar_tensor_tensor(
+                        out=prod[:], in0=acc_of[i][j][:], scalar=bl_cols[:, m : m + 1],
+                        in1=swish_of[i - STRIPS_PER_LOAD][j][:], op0=ALU.add, op1=ALU.mult,
+                    )
+                    prods.append(prod)
+                prod_of[i] = prods
+
+        def turn(i):
+            banks = []
+            for j in range(TILES_PER_STRIP):
+                turned = psum.tile([P, BATCH, P], F32, tag="bank")
+                for b in range(BATCH):
+                    nc.tensor.transpose(
+                        out=turned[:, b, :], in_=prod_of[i][j][:, b * P : (b + 1) * P], identity=ident_f32[:]
+                    )
+                banks.append(turned)
+            turned_of[i] = banks
+
+        def store(i):
+            for j in range(TILES_PER_STRIP):
+                first = column_tile(i, j) * P
+                place = first % STORE
+                if place == 0:
+                    out_sb = out_pool.tile([P, BATCH, STORE], F32)
+                    out_of[first // STORE] = out_sb
+                out_sb = out_of[first // STORE]
+                nc.scalar.copy(out=out_sb[:, :, place : place + P], in_=turned_of[i][j][:])
+                if place + P == STORE:
+                    nc.sync.dma_start(out=out_view[:, :, first + P - STORE : first + P], in_=out_sb[:])
+
+        tiles_f = F // P
+        tiles_g = G // P
+        bias_rows = const.tile([P, P], BF16)
+        nc.vector.memset(bias_rows[:], 0.0)
+        nc.sync.dma_start(out=bias_rows[0:tiles_f, :], in_=b1.rearrange("(m p) -> m p", p=P))
+        nc.sync.dma_start(out=bias_rows[tiles_f : tiles_f + tiles_g, :], in_=bg.rearrange("(m p) -> m p", p=P))
+        nc.sync.dma_start(
+            out=bias_rows[tiles_f + tiles_g : tiles_f + 2 * tiles_g, :], in_=bl.rearrange("(m p) -> m p", p=P)
+        )
+        beta_bf16 = const.tile([P, 1], BF16)
+        nc.sync.dma_start(out=beta_bf16[:], in_=beta.partition_broadcast(P))
+
+        h_raw = const.tile([P, BATCH, E], BF16)
+        nc.sync.dma_start(out=h_raw[:], in_=h_ffn.rearrange("b l e -> l b e"))
+        for s in range(RAW_BUFS):
+            load(s)
+        out_view = out.rearrange("b l n -> l b n")
+
+        ident_bf16 = const.tile([P, P], BF16)
+        make_identity(nc, ident_bf16[:])
+        ident_f32 = const.tile([P, P], F32)
+        make_identity(nc, ident_f32[:])
+
+        h_grouped = grouped_pool.tile([P, E_PASSES, TOKENS, PACK], BF16, align_bytes=64, tag="grouped")
+        for c in range(E_PASSES):
+            for b in range(BATCH):
+                h_t = psum.tile([P, PACK, P], BF16, tag="bank")
+                for t in range(PACK):
+                    k0 = c * K_PASS + t * P
+                    nc.tensor.transpose(out=h_t[:, t, :], in_=h_raw[:, b, k0 : k0 + P], identity=ident_bf16[:])
+                copy = nc.vector.tensor_copy if b % 2 == 0 else nc.scalar.copy
+                copy(out=h_grouped[:, c, b * P : (b + 1) * P, :], in_=h_t[:].rearrange("p t r -> p r t"))
+        h_words = const.tile([P, E_PASSES, TOKENS], U32, align_bytes=64)
+        h_scales = const.tile([P, E_PASSES, TOKENS], U8, align_bytes=64)
+        nc.vector.quantize_mx(
+            out=h_words[:].rearrange("p c r -> p (c r)").bitcast(FP8X4),
+            scales=h_scales[:].rearrange("p c r -> p (c r)"),
+            in_=h_grouped[:].rearrange("p c r t -> p (c r t)"),
+        )
+
+        bias_t = psum.tile([P, P], BF16, tag="bank")
+        nc.tensor.transpose(out=bias_t[:], in_=bias_rows[:], identity=ident_bf16[:])
+        bias_cols = const.tile([P, tiles_f + 2 * tiles_g], F32)
+        nc.vector.tensor_copy(out=bias_cols[:], in_=bias_t[:, 0 : tiles_f + 2 * tiles_g])
+        b1_cols = bias_cols[:, 0:tiles_f]
+        bg_cols = bias_cols[:, tiles_f : tiles_f + tiles_g]
+        bl_cols = bias_cols[:, tiles_f + tiles_g : tiles_f + 2 * tiles_g]
+        beta_col = const.tile([P, 1], F32)
+        nc.vector.tensor_copy(out=beta_col[:], in_=beta_bf16[:])
+        beta_bg_cols = const.tile([P, tiles_g], F32)
+        nc.vector.tensor_scalar_mul(out=beta_bg_cols[:], in0=bg_cols, scalar1=beta_col[:, 0:1])
+
+        u_words = const.tile([P, F_PASSES, TOKENS], U32, align_bytes=64)
+        u_scales = const.tile([P, F_PASSES, TOKENS], U8, align_bytes=64)
+
+        for step in range(n_strips + TURN_LAG):
+            if kind(step - TURN_LAG) == "lin":
+                turn(step - TURN_LAG)
+            if kind(step - FINISH_LAG) == "gate":
+                sigmoid(step - FINISH_LAG)
+            if kind(step - TURN_LAG) == "lin":
+                store(step - TURN_LAG)
+            if kind(step) != "none":
+                regroup(step)
+            if kind(step - FINISH_LAG) != "none":
+                finish(step - FINISH_LAG)
+            if kind(step - QUANTISE_LAG) != "none":
+                quantise(step - QUANTISE_LAG)
+            if kind(step - MULTIPLY_LAG) != "none":
+                multiply(step - MULTIPLY_LAG)

@@ -29,7 +29,6 @@ STRIPS_PER_LOAD = 4
 RAW = STRIPS_PER_LOAD * QUANT
 RAW_BUFS = 3
 BANKS = 8
-STORE = 512
 TILES_PER_STRIP = WORDS // F_PASSES // P
 
 QUANTISE_LAG = 1
@@ -71,7 +70,6 @@ def tile_llamaselfattentionblock_pb_kernel(tc, h_ffn, w1, b1, wg, bg, wl, bl, be
         swish_of = {}
         prod_of = {}
         turned_of = {}
-        out_of = {}
 
         def load(s):
             w, half = loads[s][1], loads[s][2]
@@ -95,11 +93,16 @@ def tile_llamaselfattentionblock_pb_kernel(tc, h_ffn, w1, b1, wg, bg, wl, bl, be
             n = WORDS // passes
             vector_passes = 0 if kind(i - FINISH_LAG) == "u" else passes // 2
             grouped = grouped_pool.tile([P, passes, n, PACK], BF16, align_bytes=64, tag="grouped")
-            for g in range(passes):
-                copy = nc.vector.tensor_copy if g < vector_passes else nc.scalar.copy
-                copy(
+            cols = slice(q * n, (q + 1) * n)
+            if vector_passes > 0:
+                nc.vector.tensor_copy(
+                    out=grouped[:, 0:vector_passes, :, :].rearrange("p g (c i) t -> p g c t i", i=4),
+                    in_=raw[:, 0 : vector_passes * PACK, cols].rearrange("p (g t) (c i) -> p g c t i", t=PACK, i=4),
+                )
+            for g in range(vector_passes, passes):
+                nc.scalar.copy(
                     out=grouped[:, g, :, :].rearrange("p (c i) t -> p c t i", i=4),
-                    in_=raw[:, g * PACK : (g + 1) * PACK, q * n : (q + 1) * n].rearrange("p t (c i) -> p c t i", i=4),
+                    in_=raw[:, g * PACK : (g + 1) * PACK, cols].rearrange("p t (c i) -> p c t i", i=4),
                 )
             grouped_of[i] = grouped
             if q == STRIPS_PER_LOAD - 1 and s + RAW_BUFS < len(loads):
@@ -224,16 +227,11 @@ def tile_llamaselfattentionblock_pb_kernel(tc, h_ffn, w1, b1, wg, bg, wl, bl, be
             turned_of[i] = banks
 
         def store(i):
+            out_sb = out_pool.tile([P, BATCH, TILES_PER_STRIP * P], F32)
             for j in range(TILES_PER_STRIP):
-                first = column_tile(i, j) * P
-                place = first % STORE
-                if place == 0:
-                    out_sb = out_pool.tile([P, BATCH, STORE], F32)
-                    out_of[first // STORE] = out_sb
-                out_sb = out_of[first // STORE]
-                nc.scalar.copy(out=out_sb[:, :, place : place + P], in_=turned_of[i][j][:])
-                if place + P == STORE:
-                    nc.sync.dma_start(out=out_view[:, :, first + P - STORE : first + P], in_=out_sb[:])
+                nc.scalar.copy(out=out_sb[:, :, j * P : (j + 1) * P], in_=turned_of[i][j][:])
+            first = column_tile(i, 0) * P
+            nc.sync.dma_start(out=out_view[:, :, first : first + TILES_PER_STRIP * P], in_=out_sb[:])
 
         tiles_f = F // P
         tiles_g = G // P
@@ -248,10 +246,15 @@ def tile_llamaselfattentionblock_pb_kernel(tc, h_ffn, w1, b1, wg, bg, wl, bl, be
         nc.sync.dma_start(out=beta_bf16[:], in_=beta.partition_broadcast(P))
 
         h_raw = const.tile([P, BATCH, E], BF16)
-        nc.sync.dma_start(out=h_raw[:], in_=h_ffn.rearrange("b l e -> l b e"))
+        for b in range(BATCH):
+            nc.sync.dma_start(out=h_raw[:, b, :], in_=h_ffn[b, :, :])
         for s in range(RAW_BUFS):
             load(s)
         out_view = out.rearrange("b l n -> l b n")
+
+        warm = const.tile([P, 1], F32)
+        nc.vector.memset(warm[:], 0.0)
+        nc.scalar.activation(out=warm[:], in_=warm[:], func=ACT.Sigmoid)
 
         ident_bf16 = const.tile([P, P], BF16)
         make_identity(nc, ident_bf16[:])

@@ -33,8 +33,10 @@ TILES_PER_STRIP = WORDS // F_PASSES // P
 
 QUANTISE_LAG = 1
 MULTIPLY_LAG = 2
+SIGMOID_LAG = 3
 FINISH_LAG = 3
 TURN_LAG = 4
+STORE_LAG = 4
 
 FLOPS = 2 * TOKENS * E * F + 2 * 2 * TOKENS * F * G
 
@@ -80,10 +82,11 @@ def tile_llamaselfattentionblock_pb_kernel(tc, h_ffn, w1, b1, wg, bg, wl, bl, be
             piece = width // cuts
             for cut in range(cuts):
                 first = half * width + cut * piece
-                nc.sync.dma_start(
-                    out=raw[:, :, cut * piece : (cut + 1) * piece],
-                    in_=w[:, first : first + piece].rearrange("(r p) n -> p r n", p=P),
-                )
+                for g in range(rows // PACK):
+                    nc.sync.dma_start(
+                        out=raw[:, g * PACK : (g + 1) * PACK, cut * piece : (cut + 1) * piece],
+                        in_=w[g * K_PASS : (g + 1) * K_PASS, first : first + piece].rearrange("(t p) n -> p t n", p=P),
+                    )
             raw_of[s] = raw
 
         def regroup(i):
@@ -293,15 +296,15 @@ def tile_llamaselfattentionblock_pb_kernel(tc, h_ffn, w1, b1, wg, bg, wl, bl, be
         u_words = const.tile([P, F_PASSES, TOKENS], U32, align_bytes=64)
         u_scales = const.tile([P, F_PASSES, TOKENS], U8, align_bytes=64)
 
-        for step in range(n_strips + TURN_LAG):
+        for step in range(n_strips + STORE_LAG):
             if kind(step - TURN_LAG) == "lin":
                 turn(step - TURN_LAG)
-            if kind(step - FINISH_LAG) == "gate":
-                sigmoid(step - FINISH_LAG)
-            if kind(step - TURN_LAG) == "lin":
-                store(step - TURN_LAG)
+            if kind(step - SIGMOID_LAG) == "gate":
+                sigmoid(step - SIGMOID_LAG)
             if kind(step) != "none":
                 regroup(step)
+            if kind(step - STORE_LAG) == "lin":
+                store(step - STORE_LAG)
             if kind(step - FINISH_LAG) != "none":
                 finish(step - FINISH_LAG)
             if kind(step - QUANTISE_LAG) != "none":

from contextlib import ExitStack

import concourse.mybir as mybir
from concourse.masks import make_identity

BF16 = mybir.dt.bfloat16
F32 = mybir.dt.float32
U32 = mybir.dt.uint32
U8 = mybir.dt.uint8
FP8X4 = mybir.dt.float8_e4m3fn_x4
ACT = mybir.ActivationFunctionType
ALU = mybir.AluOpType

P = 128
PACK = 4
K_PASS = P * PACK

BATCH = 4
TOKENS = BATCH * P
E = 1024
F = 2048
G = 2048
E_PASSES = E // K_PASS
F_PASSES = F // K_PASS

QUANT = 4096
WORDS = QUANT // PACK
STRIPS_PER_LOAD = 4
RAW = STRIPS_PER_LOAD * QUANT
RAW_BUFS = 3
BANKS = 8
TILES_PER_STRIP = WORDS // F_PASSES // P

QUANTISE_LAG = 1
MULTIPLY_LAG = 2
SIGMOID_LAG = 3
FINISH_LAG = 3
TURN_LAG = 4
STORE_LAG = 4

FLOPS = 2 * TOKENS * E * F + 2 * 2 * TOKENS * F * G


def tile_llamaselfattentionblock_pb_kernel(tc, h_ffn, w1, b1, wg, bg, wl, bl, beta, out):
    nc = tc.nc
    with ExitStack() as ctx:
        const = ctx.enter_context(tc.tile_pool(name="const", bufs=1))
        raw_pool = ctx.enter_context(tc.tile_pool(name="raw", bufs=RAW_BUFS))
        grouped_pool = ctx.enter_context(tc.tile_pool(name="grouped", bufs=3))
        strip_pool = ctx.enter_context(tc.tile_pool(name="strip", bufs=4))
        u_pool = ctx.enter_context(tc.tile_pool(name="u", bufs=2))
        swish_pool = ctx.enter_context(tc.tile_pool(name="swish", bufs=10))
        work = ctx.enter_context(tc.tile_pool(name="work", bufs=4))
        out_pool = ctx.enter_context(tc.tile_pool(name="out", bufs=2))
        psum = ctx.enter_context(tc.psum_pool(name="psum", bufs=BANKS))
        ctx.enter_context(tc.manual_schedule())
        loads = [("u", w1, 0)]
        for half in range(2):
            loads.append(("gate", wg, half))
            loads.append(("lin", wl, half))
        n_strips = len(loads) * STRIPS_PER_LOAD

        def kind(i):
            return loads[i // STRIPS_PER_LOAD][0] if 0 <= i < n_strips else "none"

        raw_of = {}
        grouped_of = {}
        words_of = {}
        scales_of = {}
        acc_of = {}
        sig_of = {}
        swish_of = {}
        prod_of = {}
        turned_of = {}

        def load(s):
            w, half = loads[s][1], loads[s][2]
            rows = w.shape[0] // P
            width = RAW // rows
            raw = raw_pool.tile([P, rows, width], BF16, tag="raw")
            cuts = max(1, STRIPS_PER_LOAD >> s)
            piece = width // cuts
            for cut in range(cuts):
                first = half * width + cut * piece
                for g in range(rows // PACK):
                    nc.sync.dma_start(
                        out=raw[:, g * PACK : (g + 1) * PACK, cut * piece : (cut + 1) * piece],
                        in_=w[g * K_PASS : (g + 1) * K_PASS, first : first + piece].rearrange("(t p) n -> p t n", p=P),
                    )
            raw_of[s] = raw

        def regroup(i):
            s, q = divmod(i, STRIPS_PER_LOAD)
            raw = raw_of[s]
            passes = raw.shape[1] // PACK
            n = WORDS // passes
            vector_passes = 0 if kind(i - FINISH_LAG) == "u" else passes // 2
            grouped = grouped_pool.tile([P, passes, n, PACK], BF16, align_bytes=64, tag="grouped")
            cols = slice(q * n, (q + 1) * n)
            if vector_passes > 0:
                nc.vector.tensor_copy(
                    out=grouped[:, 0:vector_passes, :, :].rearrange("p g (c i) t -> p g c t i", i=4),
                    in_=raw[:, 0 : vector_passes * PACK, cols].rearrange("p (g t) (c i) -> p g c t i", t=PACK, i=4),
                )
            for g in range(vector_passes, passes):
                nc.scalar.copy(
                    out=grouped[:, g, :, :].rearrange("p (c i) t -> p c t i", i=4),
                    in_=raw[:, g * PACK : (g + 1) * PACK, cols].rearrange("p t (c i) -> p c t i", i=4),
                )
            grouped_of[i] = grouped
            if q == STRIPS_PER_LOAD - 1 and s + RAW_BUFS < len(loads):
                load(s + RAW_BUFS)

        def quantise(i):
            grouped = grouped_of[i]
            passes, n = grouped.shape[1], grouped.shape[2]
            words = strip_pool.tile([P, passes, n], U32, align_bytes=64, tag="words")
            scales = strip_pool.tile([P, passes, n], U8, align_bytes=64, tag="scales")
            nc.vector.quantize_mx(
                out=words[:].rearrange("p g n -> p (g n)").bitcast(FP8X4),
                scales=scales[:].rearrange("p g n -> p (g n)"),
                in_=grouped[:].rearrange("p g n t -> p (g n t)"),
            )
            words_of[i] = words
            scales_of[i] = scales

        def column_tile(i, j):
            s, q = divmod(i, STRIPS_PER_LOAD)
            return (loads[s][2] * STRIPS_PER_LOAD + q) * TILES_PER_STRIP + j

        def multiply(i):
            words, scales = words_of[i], scales_of[i]
            banks = []
            if kind(i) == "u":
                for b in range(BATCH):
                    tokens = slice(b * P, (b + 1) * P)
                    u_acc = psum.tile([P, PACK, P], F32, tag="bank")
                    for t in range(PACK):
                        features = slice(t * P, (t + 1) * P)
                        for c in range(E_PASSES):
                            nc.tensor.matmul_mx(
                                out=u_acc[:, t, :],
                                lhsT=words[:, c, features].bitcast(FP8X4),
                                lhsT_scale=scales[:, c, features],
                                rhs=h_words[:, c, tokens].bitcast(FP8X4),
                                rhs_scale=h_scales[:, c, tokens],
                                start=(c == 0),
                                stop=(c == E_PASSES - 1),
                            )
                    banks.append(u_acc)
            else:
                for j in range(TILES_PER_STRIP):
                    cols = slice(j * P, (j + 1) * P)
                    acc = psum.tile([P, TOKENS], F32, tag="bank")
                    for g in range(F_PASSES):
                        nc.tensor.matmul_mx(
                            out=acc[:],
                            lhsT=words[:, g, cols].bitcast(FP8X4),
                            lhsT_scale=scales[:, g, cols],
                            rhs=u_words[:, g, :].bitcast(FP8X4),
                            rhs_scale=u_scales[:, g, :],
                            start=(g == 0),
                            stop=(g == F_PASSES - 1),
                        )
                    banks.append(acc)
            acc_of[i] = banks

        def sigmoid(i):
            sigs = []
            for j in range(TILES_PER_STRIP):
                m = column_tile(i, j)
                sig = work.tile([P, TOKENS], F32, tag="sig")
                nc.scalar.activation(
                    out=sig[:],
                    in_=acc_of[i][j][:],
                    func=ACT.Sigmoid,
                    bias=beta_bg_cols[:, m : m + 1],
                    scale=beta_col[:, 0:1],
                )
                sigs.append(sig)
            sig_of[i] = sigs

        def finish(i):
            if kind(i) == "u":
                u_grouped = u_pool.tile([P, TOKENS, PACK], BF16, align_bytes=64)
                for b in range(BATCH):
                    nc.vector.tensor_tensor(
                        out=u_grouped[:, b * P : (b + 1) * P, :],
                        in0=acc_of[i][b][:].rearrange("p t r -> p r t"),
                        in1=b1_cols[:, i * PACK : (i + 1) * PACK].unsqueeze(1).to_broadcast([P, P, PACK]),
                        op=ALU.add,
                    )
                nc.vector.quantize_mx(
                    out=u_words[:, i, :].bitcast(FP8X4),
                    scales=u_scales[:, i, :],
                    in_=u_grouped[:].rearrange("p r t -> p (r t)"),
                )
            elif kind(i) == "gate":
                swishes = []
                for j in range(TILES_PER_STRIP):
                    m = column_tile(i, j)
                    swish = swish_pool.tile([P, TOKENS], F32)
                    nc.vector.scalar_tensor_tensor(
                        out=swish[:], in0=acc_of[i][j][:], scalar=bg_cols[:, m : m + 1], in1=sig_of[i][j][:],
                        op0=ALU.add, op1=ALU.mult,
                    )
                    swishes.append(swish)
                swish_of[i] = swishes
            else:
                prods = []
                for j in range(TILES_PER_STRIP):
                    m = column_tile(i, j)
                    prod = work.tile([P, TOKENS], F32, tag="prod")
                    nc.vector.scalar_tensor_tensor(
                        out=prod[:], in0=acc_of[i][j][:], scalar=bl_cols[:, m : m + 1],
                        in1=swish_of[i - STRIPS_PER_LOAD][j][:], op0=ALU.add, op1=ALU.mult,
                    )
                    prods.append(prod)
                prod_of[i] = prods

        def turn(i):
            banks = []
            for j in range(TILES_PER_STRIP):
                turned = psum.tile([P, BATCH, P], F32, tag="bank")
                for b in range(BATCH):
                    nc.tensor.transpose(
                        out=turned[:, b, :], in_=prod_of[i][j][:, b * P : (b + 1) * P], identity=ident_f32[:]
                    )
                banks.append(turned)
            turned_of[i] = banks

        def store(i):
            out_sb = out_pool.tile([P, BATCH, TILES_PER_STRIP * P], F32)
            for j in range(TILES_PER_STRIP):
                nc.scalar.copy(out=out_sb[:, :, j * P : (j + 1) * P], in_=turned_of[i][j][:])
            first = column_tile(i, 0) * P
            nc.sync.dma_start(out=out_view[:, :, first : first + TILES_PER_STRIP * P], in_=out_sb[:])

        tiles_f = F // P
        tiles_g = G // P
        bias_rows = const.tile([P, P], BF16)
        nc.vector.memset(bias_rows[:], 0.0)
        nc.sync.dma_start(out=bias_rows[0:tiles_f, :], in_=b1.rearrange("(m p) -> m p", p=P))
        nc.sync.dma_start(out=bias_rows[tiles_f : tiles_f + tiles_g, :], in_=bg.rearrange("(m p) -> m p", p=P))
        nc.sync.dma_start(
            out=bias_rows[tiles_f + tiles_g : tiles_f + 2 * tiles_g, :], in_=bl.rearrange("(m p) -> m p", p=P)
        )
        beta_bf16 = const.tile([P, 1], BF16)
        nc.sync.dma_start(out=beta_bf16[:], in_=beta.partition_broadcast(P))

        h_raw = const.tile([P, BATCH, E], BF16)
        for b in range(BATCH):
            nc.sync.dma_start(out=h_raw[:, b, :], in_=h_ffn[b, :, :])
        for s in range(RAW_BUFS):
            load(s)
        out_view = out.rearrange("b l n -> l b n")

        warm = const.tile([P, 1], F32)
        nc.vector.memset(warm[:], 0.0)
        nc.scalar.activation(out=warm[:], in_=warm[:], func=ACT.Sigmoid)

        ident_bf16 = const.tile([P, P], BF16)
        make_identity(nc, ident_bf16[:])
        ident_f32 = const.tile([P, P], F32)
        make_identity(nc, ident_f32[:])

        h_grouped = grouped_pool.tile([P, E_PASSES, TOKENS, PACK], BF16, align_bytes=64, tag="grouped")
        for c in range(E_PASSES):
            for b in range(BATCH):
                h_t = psum.tile([P, PACK, P], BF16, tag="bank")
                for t in range(PACK):
                    k0 = c * K_PASS + t * P
                    nc.tensor.transpose(out=h_t[:, t, :], in_=h_raw[:, b, k0 : k0 + P], identity=ident_bf16[:])
                copy = nc.vector.tensor_copy if b % 2 == 0 else nc.scalar.copy
                copy(out=h_grouped[:, c, b * P : (b + 1) * P, :], in_=h_t[:].rearrange("p t r -> p r t"))
        h_words = const.tile([P, E_PASSES, TOKENS], U32, align_bytes=64)
        h_scales = const.tile([P, E_PASSES, TOKENS], U8, align_bytes=64)
        nc.vector.quantize_mx(
            out=h_words[:].rearrange("p c r -> p (c r)").bitcast(FP8X4),
            scales=h_scales[:].rearrange("p c r -> p (c r)"),
            in_=h_grouped[:].rearrange("p c r t -> p (c r t)"),
        )

        bias_t = psum.tile([P, P], BF16, tag="bank")
        nc.tensor.transpose(out=bias_t[:], in_=bias_rows[:], identity=ident_bf16[:])
        bias_cols = const.tile([P, tiles_f + 2 * tiles_g], F32)
        nc.vector.tensor_copy(out=bias_cols[:], in_=bias_t[:, 0 : tiles_f + 2 * tiles_g])
        b1_cols = bias_cols[:, 0:tiles_f]
        bg_cols = bias_cols[:, tiles_f : tiles_f + tiles_g]
        bl_cols = bias_cols[:, tiles_f + tiles_g : tiles_f + 2 * tiles_g]
        beta_col = const.tile([P, 1], F32)
        nc.vector.tensor_copy(out=beta_col[:], in_=beta_bf16[:])
        beta_bg_cols = const.tile([P, tiles_g], F32)
        nc.vector.tensor_scalar_mul(out=beta_bg_cols[:], in0=bg_cols, scalar1=beta_col[:, 0:1])

        u_words = const.tile([P, F_PASSES, TOKENS], U32, align_bytes=64)
        u_scales = const.tile([P, F_PASSES, TOKENS], U8, align_bytes=64)

        for step in range(n_strips + STORE_LAG):
            if kind(step - TURN_LAG) == "lin":
                turn(step - TURN_LAG)
            if kind(step - SIGMOID_LAG) == "gate":
                sigmoid(step - SIGMOID_LAG)
            if kind(step) != "none":
                regroup(step)
            if kind(step - STORE_LAG) == "lin":
                store(step - STORE_LAG)
            if kind(step - FINISH_LAG) != "none":
                finish(step - FINISH_LAG)
            if kind(step - QUANTISE_LAG) != "none":
                quantise(step - QUANTISE_LAG)
            if kind(step - MULTIPLY_LAG) != "none":
                multiply(step - MULTIPLY_LAG)
